import numpy as np
import ml_dtypes


def mxq(x, axis, fmt="e4m3"):
    dtype, down = {"e4m3": (ml_dtypes.float8_e4m3fn, 7), "e5m2": (ml_dtypes.float8_e5m2, 14)}[fmt]
    v = np.moveaxis(np.asarray(x, np.float32).astype(ml_dtypes.bfloat16).astype(np.float64), axis, -1)
    blocks = v.reshape(v.shape[:-1] + (-1, 32))
    amax = np.abs(blocks).max(-1, keepdims=True)
    byte = np.maximum(np.where(amax > 0, np.frexp(amax)[1] - 1 + 127, 0) - down, 1)
    scale = np.exp2(byte - 127.0)
    codes = (blocks / scale).astype(np.float32).astype(dtype).astype(np.float64)
    return np.moveaxis((codes * scale).reshape(v.shape), -1, axis)


WIDE = False


def mx_kscale(k):
    if not WIDE:
        return np.ones(k)
    levels = np.array([20, -20, 10, -10, 0])
    a = np.random.permutation(np.resize(levels, k // 512 * 4)).reshape(k // 512, 4)
    idx = np.arange(k)
    return np.exp2(a[idx // 512, idx % 128 // 32])


BF16 = ml_dtypes.bfloat16


def bf(x):
    return np.asarray(x, np.float32).astype(BF16)


def f64(x):
    return np.asarray(x).astype(np.float64)


S, B, SC = 2048, 1024, 1024
MARGIN = 1.0 / 64.0


def _cm(p, av, al):
    over_avail = (av[None, :] - p < 0.0) & (p > 0.0)
    over_alloc = (al[None, :] + p < 0.0) & (p < 0.0)
    return np.where(over_avail | over_alloc, 0.01, 1.0)


def setup_inputs():
    u = mx_kscale(SC)
    p = f64(bf(np.random.standard_normal((S, B))))
    cur = np.random.random_sample((S, SC))
    bun = np.random.random_sample((B, SC)) * (16.0 / np.sqrt(B)) / u
    av = f64(bf(np.random.random_sample(B)))
    al = f64(bf(np.random.random_sample(B)))
    g = np.random.standard_normal((S, SC)) * np.exp2(np.random.randint(-12, 1, (S, 1))) * u
    near = (np.abs(p - av[None, :]) < MARGIN) | (np.abs(p + al[None, :]) < MARGIN)
    p = np.where(near, np.where(p < 0.0, -2.0, 2.0), p)
    return {"proba": bf(p.reshape(-1)),
            "cur_inven": bf(cur),
            "bun_sc": bf(bun),
            "avail_bundle": bf(av),
            "alloc_bundle": bf(al),
            "grad_out": bf(g.reshape(1, -1))}


def reference(proba, cur_inven, bun_sc, avail_bundle, alloc_bundle, grad_out):
    p = f64(proba).reshape(S, B)
    cm = _cm(p, f64(avail_bundle), f64(alloc_bundle))
    g = f64(grad_out).reshape(S, SC)
    gh = mxq(g, 1, "e5m2") @ mxq(f64(bun_sc), 1, "e4m3").T
    return (gh * cm).reshape(-1)

@@ -1,0 +1,187 @@
+from contextlib import ExitStack
+
+import concourse.bass as bass
+import concourse.mybir as mybir
+import concourse.tile as tile
+from concourse.masks import make_identity
+
+F32 = mybir.dt.float32
+BF16 = mybir.dt.bfloat16
+U32 = mybir.dt.uint32
+U8 = mybir.dt.uint8
+E4X4 = mybir.dt.float8_e4m3fn_x4
+E5X4 = mybir.dt.float8_e5m2_x4
+ALU = mybir.AluOpType
+ACT = mybir.ActivationFunctionType
+
+P = 128
+S = 2048
+B = 1024
+K = 1024
+T = S // P
+NPAIR = T // 2
+NBT = B // P
+HALF = 512
+
+FLOPS = 2 * S * B * K
+BYTES = 2 * S * B + 2 * B * K + 2 * S * K + 4 * B + 4 * S * B
+
+
+def tile_optblockv2_t_kernel(
+    tc, proba, cur_inven, bun_sc, avail_bundle, alloc_bundle, grad_out, out
+):
+    nc = tc.nc
+    g_v = grad_out.rearrange("o (p x) -> (o p) x", p=P)
+    p_v = proba.rearrange("(p x) -> p x", p=P)
+    o_v = out.rearrange("(p x) -> p x", p=P)
+    bun_v = bun_sc.rearrange("(t p) k -> p t k", p=P)
+
+    with ExitStack() as ctx:
+        const = ctx.enter_context(tc.tile_pool(name="const", bufs=1))
+        res = ctx.enter_context(tc.tile_pool(name="res", bufs=1))
+        work = ctx.enter_context(tc.tile_pool(name="work", bufs=3))
+        epool = ctx.enter_context(tc.tile_pool(name="epool", bufs=8))
+        opool = ctx.enter_context(tc.tile_pool(name="opool", bufs=4))
+        psum_t = ctx.enter_context(tc.psum_pool(name="psum_t", bufs=2))
+        psum_a = ctx.enter_context(tc.psum_pool(name="psum_a", bufs=4))
+
+        zrow = const.tile([P, 2 * B], BF16, name="zrow")
+        nc.vector.memset(zrow[:], 0.0)
+        ones = const.tile([P, P], BF16, name="ones")
+        nc.vector.memset(ones[:], 1.0)
+        ident = const.tile([P, P], F32, name="ident")
+        make_identity(nc, ident[:])
+        nc.sync.dma_start(out=zrow[0:1, 0:B], in_=avail_bundle.rearrange("(o n) -> o n", o=1))
+        nc.sync.dma_start(out=zrow[0:1, B : 2 * B], in_=alloc_bundle.rearrange("(o n) -> o n", o=1))
+
+        p_sb = []
+        g_sb = []
+        bun_sb = []
+        for i in range(NPAIR):
+            p_sb.append(res.tile([P, 2 * B], BF16, name="p%d" % i))
+            g_sb.append(res.tile([P, 2 * K], BF16, name="g%d" % i))
+        for i in range(NBT // 2):
+            bun_sb.append(res.tile([P, 2, K], BF16, name="bun%d" % i))
+
+        def load_p(i):
+            nc.sync.dma_start(out=p_sb[i][:], in_=p_v[:, 2 * B * i : 2 * B * (i + 1)])
+
+        def load_g(i):
+            nc.sync.dma_start(out=g_sb[i][:], in_=g_v[:, 2 * K * i : 2 * K * (i + 1)])
+
+        load_p(0)
+        for i in range(NBT // 2):
+            nc.sync.dma_start(out=bun_sb[i][:], in_=bun_v[:, 2 * i : 2 * i + 2, :])
+        load_g(0)
+        for i in range(1, NPAIR):
+            load_p(i)
+            load_g(i)
+
+        hi = const.tile([P, B], BF16, name="hi")
+        lo = const.tile([P, B], BF16, name="lo")
+        for j in (2, 3, 0, 1):
+            th = psum_a.tile([P, HALF], F32, name="acc")
+            nc.tensor.matmul(th[:], lhsT=ones[:], rhs=zrow[:, j * HALF : (j + 1) * HALF], start=True, stop=True)
+            if j < 2:
+                nc.scalar.activation(out=hi[:, j * HALF : (j + 1) * HALF], in_=th[:], func=ACT.Relu)
+            else:
+                nc.vector.tensor_scalar(
+                    out=lo[:, (j - 2) * HALF : (j - 1) * HALF], in0=th[:],
+                    scalar1=-1.0, scalar2=0.0, op0=ALU.mult, op1=ALU.min,
+                )
+
+        e_sb = {}
+
+        def masks(i):
+            ab = []
+            for tt in range(2):
+                pt = p_sb[i][:, tt * B : (tt + 1) * B]
+                a = work.tile([P, B], BF16, name="a%d" % tt)
+                b = work.tile([P, B], BF16, name="b%d" % tt)
+                nc.vector.tensor_tensor(out=a[:], in0=pt, in1=hi[:], op=ALU.is_le)
+                nc.vector.tensor_tensor(out=b[:], in0=pt, in1=lo[:], op=ALU.is_ge)
+                ab.append((a, b))
+            for tt in range(2):
+                e = epool.tile([P, B], BF16, name="e")
+                nc.vector.tensor_tensor(out=e[:], in0=ab[tt][0][:], in1=ab[tt][1][:], op=ALU.mult)
+                e_sb[2 * i + tt] = e
+
+        gb = res.tile([P, 2 * B * 4], BF16, name="gb", align_bytes=64)
+        gbw = gb[:].bitcast(F32).rearrange("p (c b u) -> p c b u", c=2, b=B, u=2)
+        cb = res.tile([P, 2 * B], U32, name="cb", align_bytes=64)
+        sb = res.tile([P, 2 * B], U8, name="sb", align_bytes=64)
+
+        def turn(words):
+            xt = psum_t.tile([P, 4 * P], F32, name="xt")
+            for j in range(4):
+                nc.tensor.transpose(xt[:, j * P : (j + 1) * P], words[:, j * P : (j + 1) * P], ident[:])
+            return xt[:].rearrange("p (c u w) -> p c w u", c=2, u=2, w=P)
+
+        def bun_prep():
+            for bt in range(NBT):
+                words = bun_sb[bt // 2][:, bt % 2, :].bitcast(F32)
+                src = turn(words)
+                nc.scalar.copy(out=gbw[:, :, bt * P : (bt + 1) * P, :], in_=src)
+                if bt % 4 == 3:
+                    h = bt // 4
+                    for c in range(2):
+                        col = c * B + h * HALF
+                        nc.vector.quantize_mx(
+                            out=cb[:, col : col + HALF].bitcast(E4X4),
+                            scales=sb[:, col : col + HALF],
+                            in_=gb[:, 4 * col : 4 * (col + HALF)],
+                        )
+
+        cg_sb = {}
+
+        def g_prep(i):
+            gg = work.tile([P, 2 * K], BF16, name="gg", align_bytes=64)
+            ggw = gg[:].bitcast(F32)
+            gw = g_sb[i][:].bitcast(F32)
+            for tt in range(2):
+                src = turn(gw[:, tt * HALF : (tt + 1) * HALF])
+                nc.scalar.copy(
+                    out=ggw[:, tt * HALF : (tt + 1) * HALF].rearrange("p (c w u) -> p c w u", c=2, w=P, u=2),
+                    in_=src,
+                )
+            cg = work.tile([P, HALF], U32, name="cg", align_bytes=64)
+            sg = work.tile([P, HALF], U8, name="sg", align_bytes=64)
+            nc.vector.quantize_mx(out=cg[:].bitcast(E5X4), scales=sg[:], in_=gg[:])
+            cg_sb[i] = (cg, sg)
+
+        def mm_final(t):
+            cg, sg = cg_sb[t // 2]
+            o = opool.tile([P, B], F32, name="o")
+            for h in range(2):
+                acc = psum_a.tile([P, HALF], F32, name="acc")
+                for c in range(2):
+                    lc = ((t % 2) * 2 + c) * P
+                    rc = c * B + h * HALF
+                    nc.tensor.matmul_mx(
+                        out=acc[:],
+                        lhsT=cg[:, lc : lc + P].bitcast(E5X4),
+                        lhsT_scale=sg[:, lc : lc + P],
+                        rhs=cb[:, rc : rc + HALF].bitcast(E4X4),
+                        rhs_scale=sb[:, rc : rc + HALF],
+                        start=(c == 0),
+                        stop=(c == 1),
+                    )
+                nc.vector.scalar_tensor_tensor(
+                    out=o[:, h * HALF : (h + 1) * HALF],
+                    in0=e_sb[t][:, h * HALF : (h + 1) * HALF],
+                    scalar=0.01,
+                    in1=acc[:],
+                    op0=ALU.max,
+                    op1=ALU.mult,
+                )
+            nc.sync.dma_start(out=o_v[:, t * B : (t + 1) * B], in_=o[:])
+
+        masks(0)
+        bun_prep()
+        g_prep(0)
+        for i in range(NPAIR):
+            if i + 1 < NPAIR:
+                g_prep(i + 1)
+                masks(i + 1)
+            mm_final(2 * i)
+            mm_final(2 * i + 1)

@@ -1,8 +1,6 @@
 from contextlib import ExitStack
 
-import concourse.bass as bass
 import concourse.mybir as mybir
-import concourse.tile as tile
 from concourse.masks import make_identity
 
 F32 = mybir.dt.float32
@@ -22,6 +20,9 @@ T = S // P
 NPAIR = T // 2
 NBT = B // P
 HALF = 512
+GT = 4
+NG = T // GT
+MG = (1, 2, 3)
 
 FLOPS = 2 * S * B * K
 BYTES = 2 * S * B + 2 * B * K + 2 * S * K + 4 * B + 4 * S * B
@@ -40,19 +41,26 @@ def tile_optblockv2_t_kernel(
         const = ctx.enter_context(tc.tile_pool(name="const", bufs=1))
         res = ctx.enter_context(tc.tile_pool(name="res", bufs=1))
         work = ctx.enter_context(tc.tile_pool(name="work", bufs=3))
+        mpool = ctx.enter_context(tc.tile_pool(name="mpool", bufs=2))
         epool = ctx.enter_context(tc.tile_pool(name="epool", bufs=8))
         opool = ctx.enter_context(tc.tile_pool(name="opool", bufs=4))
-        psum_t = ctx.enter_context(tc.psum_pool(name="psum_t", bufs=2))
+        psum_t = ctx.enter_context(tc.psum_pool(name="psum_t", bufs=4))
         psum_a = ctx.enter_context(tc.psum_pool(name="psum_a", bufs=4))
 
         zrow = const.tile([P, 2 * B], BF16, name="zrow")
         nc.vector.memset(zrow[:], 0.0)
+        rows = const.tile([P, P], BF16, name="rows")
+        nc.vector.memset(rows[:], 0.0)
         ones = const.tile([P, P], BF16, name="ones")
         nc.vector.memset(ones[:], 1.0)
         ident = const.tile([P, P], F32, name="ident")
         make_identity(nc, ident[:])
+        identb = const.tile([P, P], BF16, name="identb")
+        make_identity(nc, identb[:])
         nc.sync.dma_start(out=zrow[0:1, 0:B], in_=avail_bundle.rearrange("(o n) -> o n", o=1))
         nc.sync.dma_start(out=zrow[0:1, B : 2 * B], in_=alloc_bundle.rearrange("(o n) -> o n", o=1))
+        nc.sync.dma_start(out=rows[0:NBT, :], in_=avail_bundle.rearrange("(t p) -> t p", p=P))
+        nc.sync.dma_start(out=rows[NBT : 2 * NBT, :], in_=alloc_bundle.rearrange("(t p) -> t p", p=P))
 
         p_sb = []
         g_sb = []
@@ -70,12 +78,16 @@ def tile_optblockv2_t_kernel(
             nc.sync.dma_start(out=g_sb[i][:], in_=g_v[:, 2 * K * i : 2 * K * (i + 1)])
 
         load_p(0)
+        load_p(1)
         for i in range(NBT // 2):
             nc.sync.dma_start(out=bun_sb[i][:], in_=bun_v[:, 2 * i : 2 * i + 2, :])
         load_g(0)
-        for i in range(1, NPAIR):
+        load_g(1)
+        for i in range(2, NPAIR, 2):
             load_p(i)
+            load_p(i + 1)
             load_g(i)
+            load_g(i + 1)
 
         hi = const.tile([P, B], BF16, name="hi")
         lo = const.tile([P, B], BF16, name="lo")
@@ -89,15 +101,26 @@ def tile_optblockv2_t_kernel(
                     out=lo[:, (j - 2) * HALF : (j - 1) * HALF], in0=th[:],
                     scalar1=-1.0, scalar2=0.0, op0=ALU.mult, op1=ALU.min,
                 )
+        rt = psum_t.tile([P, P], BF16, name="tp")
+        nc.tensor.transpose(rt[:], rows[:], identb[:])
+        hi_c = const.tile([P, NBT], F32, name="hi_c")
+        lo_c = const.tile([P, NBT], F32, name="lo_c")
+        nc.vector.tensor_scalar_max(out=hi_c[:], in0=rt[:, 0:NBT], scalar1=0.0)
+        nc.vector.tensor_scalar(
+            out=lo_c[:], in0=rt[:, NBT : 2 * NBT], scalar1=-1.0, scalar2=0.0, op0=ALU.mult, op1=ALU.min
+        )
 
         e_sb = {}
 
-        def masks(i):
+        def p_tile(t):
+            return p_sb[t // 2][:, (t % 2) * B : (t % 2 + 1) * B]
+
+        def masks_s(i):
             ab = []
             for tt in range(2):
-                pt = p_sb[i][:, tt * B : (tt + 1) * B]
-                a = work.tile([P, B], BF16, name="a%d" % tt)
-                b = work.tile([P, B], BF16, name="b%d" % tt)
+                pt = p_tile(2 * i + tt)
+                a = mpool.tile([P, B], BF16, name="a%d" % tt)
+                b = mpool.tile([P, B], BF16, name="b%d" % tt)
                 nc.vector.tensor_tensor(out=a[:], in0=pt, in1=hi[:], op=ALU.is_le)
                 nc.vector.tensor_tensor(out=b[:], in0=pt, in1=lo[:], op=ALU.is_ge)
                 ab.append((a, b))
@@ -106,13 +129,41 @@ def tile_optblockv2_t_kernel(
                 nc.vector.tensor_tensor(out=e[:], in0=ab[tt][0][:], in1=ab[tt][1][:], op=ALU.mult)
                 e_sb[2 * i + tt] = e
 
+        c_sb = {}
+
+        def clamp_t(gr):
+            p_t = mpool.tile([P, NBT, GT * P], BF16, name="p_t")
+            c_t = mpool.tile([P, NBT, GT * P], BF16, name="c_t")
+            for bt in range(NBT):
+                tp = psum_t.tile([P, GT * P], BF16, name="tp")
+                for st in range(GT):
+                    nc.tensor.transpose(
+                        tp[:, st * P : (st + 1) * P], p_tile(GT * gr + st)[:, bt * P : (bt + 1) * P], identb[:]
+                    )
+                nc.scalar.copy(out=p_t[:, bt, :], in_=tp[:])
+                nc.vector.tensor_scalar(
+                    out=c_t[:, bt, :], in0=p_t[:, bt, :],
+                    scalar1=lo_c[:, bt : bt + 1], scalar2=hi_c[:, bt : bt + 1], op0=ALU.max, op1=ALU.min,
+                )
+            c_sb[gr] = c_t
+
+        def masks_back(gr):
+            c_t = c_sb[gr]
+            for st in range(GT):
+                tp = psum_t.tile([P, B], BF16, name="tp")
+                for bt in range(NBT):
+                    nc.tensor.transpose(tp[:, bt * P : (bt + 1) * P], c_t[:, bt, st * P : (st + 1) * P], identb[:])
+                e = epool.tile([P, B], BF16, name="e")
+                nc.vector.tensor_tensor(out=e[:], in0=tp[:], in1=p_tile(GT * gr + st), op=ALU.is_equal)
+                e_sb[GT * gr + st] = e
+
         gb = res.tile([P, 2 * B * 4], BF16, name="gb", align_bytes=64)
         gbw = gb[:].bitcast(F32).rearrange("p (c b u) -> p c b u", c=2, b=B, u=2)
         cb = res.tile([P, 2 * B], U32, name="cb", align_bytes=64)
         sb = res.tile([P, 2 * B], U8, name="sb", align_bytes=64)
 
         def turn(words):
-            xt = psum_t.tile([P, 4 * P], F32, name="xt")
+            xt = psum_t.tile([P, 4 * P], F32, name="tp")
             for j in range(4):
                 nc.tensor.transpose(xt[:, j * P : (j + 1) * P], words[:, j * P : (j + 1) * P], ident[:])
             return xt[:].rearrange("p (c u w) -> p c w u", c=2, u=2, w=P)
@@ -176,12 +227,28 @@ def tile_optblockv2_t_kernel(
                 )
             nc.sync.dma_start(out=o_v[:, t * B : (t + 1) * B], in_=o[:])
 
-        masks(0)
+        def masks_first(gr):
+            if gr in MG:
+                clamp_t(gr)
+            else:
+                masks_s(2 * gr)
+                masks_s(2 * gr + 1)
+
+        masks_first(0)
         bun_prep()
         g_prep(0)
-        for i in range(NPAIR):
-            if i + 1 < NPAIR:
-                g_prep(i + 1)
-                masks(i + 1)
-            mm_final(2 * i)
-            mm_final(2 * i + 1)
+        g_prep(1)
+        if 0 in MG:
+            masks_back(0)
+        for gr in range(NG):
+            nxt = gr + 1
+            if nxt < NG:
+                masks_first(nxt)
+                g_prep(2 * nxt)
+                g_prep(2 * nxt + 1)
+            mm_final(GT * gr)
+            mm_final(GT * gr + 1)
+            if nxt < NG and nxt in MG:
+                masks_back(nxt)
+            mm_final(GT * gr + 2)
+            mm_final(GT * gr + 3)

@@ -10,7 +10,6 @@ U8 = mybir.dt.uint8
 E4X4 = mybir.dt.float8_e4m3fn_x4
 E5X4 = mybir.dt.float8_e5m2_x4
 ALU = mybir.AluOpType
-ACT = mybir.ActivationFunctionType
 
 P = 128
 S = 2048
@@ -22,7 +21,6 @@ NBT = B // P
 HALF = 512
 GT = 4
 NG = T // GT
-MG = (1, 2, 3)
 
 FLOPS = 2 * S * B * K
 BYTES = 2 * S * B + 2 * B * K + 2 * S * K + 4 * B + 4 * S * B
@@ -43,22 +41,17 @@ def tile_optblockv2_t_kernel(
         work = ctx.enter_context(tc.tile_pool(name="work", bufs=3))
         mpool = ctx.enter_context(tc.tile_pool(name="mpool", bufs=2))
         epool = ctx.enter_context(tc.tile_pool(name="epool", bufs=8))
-        opool = ctx.enter_context(tc.tile_pool(name="opool", bufs=4))
+        opool = ctx.enter_context(tc.tile_pool(name="opool", bufs=6))
         psum_t = ctx.enter_context(tc.psum_pool(name="psum_t", bufs=4))
         psum_a = ctx.enter_context(tc.psum_pool(name="psum_a", bufs=4))
+        ctx.enter_context(tc.manual_schedule())
 
-        zrow = const.tile([P, 2 * B], BF16, name="zrow")
-        nc.vector.memset(zrow[:], 0.0)
         rows = const.tile([P, P], BF16, name="rows")
         nc.vector.memset(rows[:], 0.0)
-        ones = const.tile([P, P], BF16, name="ones")
-        nc.vector.memset(ones[:], 1.0)
-        ident = const.tile([P, P], F32, name="ident")
-        make_identity(nc, ident[:])
         identb = const.tile([P, P], BF16, name="identb")
         make_identity(nc, identb[:])
-        nc.sync.dma_start(out=zrow[0:1, 0:B], in_=avail_bundle.rearrange("(o n) -> o n", o=1))
-        nc.sync.dma_start(out=zrow[0:1, B : 2 * B], in_=alloc_bundle.rearrange("(o n) -> o n", o=1))
+        ident = const.tile([P, P], F32, name="ident")
+        make_identity(nc, ident[:])
         nc.sync.dma_start(out=rows[0:NBT, :], in_=avail_bundle.rearrange("(t p) -> t p", p=P))
         nc.sync.dma_start(out=rows[NBT : 2 * NBT, :], in_=alloc_bundle.rearrange("(t p) -> t p", p=P))
 
@@ -82,25 +75,13 @@ def tile_optblockv2_t_kernel(
         for i in range(NBT // 2):
             nc.sync.dma_start(out=bun_sb[i][:], in_=bun_v[:, 2 * i : 2 * i + 2, :])
         load_g(0)
-        load_g(1)
-        for i in range(2, NPAIR, 2):
-            load_p(i)
-            load_p(i + 1)
-            load_g(i)
-            load_g(i + 1)
+        for gr in range(1, NG):
+            load_p(2 * gr)
+            load_p(2 * gr + 1)
+            load_g(2 * gr - 1)
+            load_g(2 * gr)
+        load_g(NPAIR - 1)
 
-        hi = const.tile([P, B], BF16, name="hi")
-        lo = const.tile([P, B], BF16, name="lo")
-        for j in (2, 3, 0, 1):
-            th = psum_a.tile([P, HALF], F32, name="acc")
-            nc.tensor.matmul(th[:], lhsT=ones[:], rhs=zrow[:, j * HALF : (j + 1) * HALF], start=True, stop=True)
-            if j < 2:
-                nc.scalar.activation(out=hi[:, j * HALF : (j + 1) * HALF], in_=th[:], func=ACT.Relu)
-            else:
-                nc.vector.tensor_scalar(
-                    out=lo[:, (j - 2) * HALF : (j - 1) * HALF], in0=th[:],
-                    scalar1=-1.0, scalar2=0.0, op0=ALU.mult, op1=ALU.min,
-                )
         rt = psum_t.tile([P, P], BF16, name="tp")
         nc.tensor.transpose(rt[:], rows[:], identb[:])
         hi_c = const.tile([P, NBT], F32, name="hi_c")
@@ -110,145 +91,175 @@ def tile_optblockv2_t_kernel(
             out=lo_c[:], in0=rt[:, NBT : 2 * NBT], scalar1=-1.0, scalar2=0.0, op0=ALU.mult, op1=ALU.min
         )
 
-        e_sb = {}
-
         def p_tile(t):
             return p_sb[t // 2][:, (t % 2) * B : (t % 2 + 1) * B]
 
-        def masks_s(i):
-            ab = []
-            for tt in range(2):
-                pt = p_tile(2 * i + tt)
-                a = mpool.tile([P, B], BF16, name="a%d" % tt)
-                b = mpool.tile([P, B], BF16, name="b%d" % tt)
-                nc.vector.tensor_tensor(out=a[:], in0=pt, in1=hi[:], op=ALU.is_le)
-                nc.vector.tensor_tensor(out=b[:], in0=pt, in1=lo[:], op=ALU.is_ge)
-                ab.append((a, b))
-            for tt in range(2):
-                e = epool.tile([P, B], BF16, name="e")
-                nc.vector.tensor_tensor(out=e[:], in0=ab[tt][0][:], in1=ab[tt][1][:], op=ALU.mult)
-                e_sb[2 * i + tt] = e
+        def copy_out(on_vector, dst, src):
+            if on_vector:
+                nc.vector.tensor_copy(out=dst, in_=src)
+            else:
+                nc.scalar.copy(out=dst, in_=src)
 
-        c_sb = {}
+        pt_sb = {}
+        ct_sb = {}
+        tc_ps = {}
+        e_sb = {}
+        gg_sb = {}
+        cg_sb = {}
+        acc_ps = {}
+        o_sb = {}
 
-        def clamp_t(gr):
-            p_t = mpool.tile([P, NBT, GT * P], BF16, name="p_t")
-            c_t = mpool.tile([P, NBT, GT * P], BF16, name="c_t")
-            for bt in range(NBT):
-                tp = psum_t.tile([P, GT * P], BF16, name="tp")
-                for st in range(GT):
-                    nc.tensor.transpose(
-                        tp[:, st * P : (st + 1) * P], p_tile(GT * gr + st)[:, bt * P : (bt + 1) * P], identb[:]
-                    )
-                nc.scalar.copy(out=p_t[:, bt, :], in_=tp[:])
-                nc.vector.tensor_scalar(
-                    out=c_t[:, bt, :], in0=p_t[:, bt, :],
-                    scalar1=lo_c[:, bt : bt + 1], scalar2=hi_c[:, bt : bt + 1], op0=ALU.max, op1=ALU.min,
-                )
-            c_sb[gr] = c_t
-
-        def masks_back(gr):
-            c_t = c_sb[gr]
+        def turn_p(gr, bt, on_vector=False):
+            if bt == 0:
+                pt_sb[gr] = mpool.tile([P, NBT, GT * P], BF16, name="p_t")
+                ct_sb[gr] = mpool.tile([P, NBT, GT * P], BF16, name="c_t")
+            tp = psum_t.tile([P, GT * P], BF16, name="tp")
             for st in range(GT):
-                tp = psum_t.tile([P, B], BF16, name="tp")
-                for bt in range(NBT):
-                    nc.tensor.transpose(tp[:, bt * P : (bt + 1) * P], c_t[:, bt, st * P : (st + 1) * P], identb[:])
-                e = epool.tile([P, B], BF16, name="e")
-                nc.vector.tensor_tensor(out=e[:], in0=tp[:], in1=p_tile(GT * gr + st), op=ALU.is_equal)
-                e_sb[GT * gr + st] = e
+                nc.tensor.transpose(
+                    tp[:, st * P : (st + 1) * P], p_tile(GT * gr + st)[:, bt * P : (bt + 1) * P], identb[:]
+                )
+            copy_out(on_vector, pt_sb[gr][:, bt, :], tp[:])
+
+        def clamp(gr, bt):
+            nc.vector.tensor_scalar(
+                out=ct_sb[gr][:, bt, :], in0=pt_sb[gr][:, bt, :],
+                scalar1=lo_c[:, bt : bt + 1], scalar2=hi_c[:, bt : bt + 1], op0=ALU.max, op1=ALU.min,
+            )
+
+        def turn_back(t):
+            c_t = ct_sb[t // GT]
+            st = t % GT
+            tp = psum_t.tile([P, B], BF16, name="tp")
+            for bt in range(NBT):
+                nc.tensor.transpose(tp[:, bt * P : (bt + 1) * P], c_t[:, bt, st * P : (st + 1) * P], identb[:])
+            tc_ps[t] = tp
+
+        def in_range(t):
+            e = epool.tile([P, B], BF16, name="e")
+            nc.vector.tensor_tensor(out=e[:], in0=tc_ps[t][:], in1=p_tile(t), op=ALU.is_equal)
+            e_sb[t] = e
 
         gb = res.tile([P, 2 * B * 4], BF16, name="gb", align_bytes=64)
         gbw = gb[:].bitcast(F32).rearrange("p (c b u) -> p c b u", c=2, b=B, u=2)
         cb = res.tile([P, 2 * B], U32, name="cb", align_bytes=64)
         sb = res.tile([P, 2 * B], U8, name="sb", align_bytes=64)
 
-        def turn(words):
+        def turn_words(words):
             xt = psum_t.tile([P, 4 * P], F32, name="tp")
             for j in range(4):
                 nc.tensor.transpose(xt[:, j * P : (j + 1) * P], words[:, j * P : (j + 1) * P], ident[:])
             return xt[:].rearrange("p (c u w) -> p c w u", c=2, u=2, w=P)
 
-        def bun_prep():
-            for bt in range(NBT):
-                words = bun_sb[bt // 2][:, bt % 2, :].bitcast(F32)
-                src = turn(words)
-                nc.scalar.copy(out=gbw[:, :, bt * P : (bt + 1) * P, :], in_=src)
-                if bt % 4 == 3:
-                    h = bt // 4
-                    for c in range(2):
-                        col = c * B + h * HALF
-                        nc.vector.quantize_mx(
-                            out=cb[:, col : col + HALF].bitcast(E4X4),
-                            scales=sb[:, col : col + HALF],
-                            in_=gb[:, 4 * col : 4 * (col + HALF)],
-                        )
+        def turn_bun(bt, on_vector):
+            src = turn_words(bun_sb[bt // 2][:, bt % 2, :].bitcast(F32))
+            copy_out(on_vector, gbw[:, :, bt * P : (bt + 1) * P, :], src)
 
-        cg_sb = {}
-
-        def g_prep(i):
-            gg = work.tile([P, 2 * K], BF16, name="gg", align_bytes=64)
-            ggw = gg[:].bitcast(F32)
-            gw = g_sb[i][:].bitcast(F32)
-            for tt in range(2):
-                src = turn(gw[:, tt * HALF : (tt + 1) * HALF])
-                nc.scalar.copy(
-                    out=ggw[:, tt * HALF : (tt + 1) * HALF].rearrange("p (c w u) -> p c w u", c=2, w=P, u=2),
-                    in_=src,
+        def quant_bun(h):
+            for c in range(2):
+                col = c * B + h * HALF
+                nc.vector.quantize_mx(
+                    out=cb[:, col : col + HALF].bitcast(E4X4),
+                    scales=sb[:, col : col + HALF],
+                    in_=gb[:, 4 * col : 4 * (col + HALF)],
                 )
+
+        def turn_g(t, on_vector=False):
+            i = t // 2
+            tt = t % 2
+            if tt == 0:
+                gg_sb[i] = work.tile([P, 2 * K], BF16, name="gg", align_bytes=64)
+            src = turn_words(g_sb[i][:].bitcast(F32)[:, tt * HALF : (tt + 1) * HALF])
+            dst = gg_sb[i][:].bitcast(F32)[:, tt * HALF : (tt + 1) * HALF]
+            copy_out(on_vector, dst.rearrange("p (c w u) -> p c w u", c=2, w=P, u=2), src)
+
+        def quant_g(i):
             cg = work.tile([P, HALF], U32, name="cg", align_bytes=64)
             sg = work.tile([P, HALF], U8, name="sg", align_bytes=64)
-            nc.vector.quantize_mx(out=cg[:].bitcast(E5X4), scales=sg[:], in_=gg[:])
+            nc.vector.quantize_mx(out=cg[:].bitcast(E5X4), scales=sg[:], in_=gg_sb[i][:])
             cg_sb[i] = (cg, sg)
 
-        def mm_final(t):
+        def multiply(t, h):
             cg, sg = cg_sb[t // 2]
-            o = opool.tile([P, B], F32, name="o")
-            for h in range(2):
-                acc = psum_a.tile([P, HALF], F32, name="acc")
-                for c in range(2):
-                    lc = ((t % 2) * 2 + c) * P
-                    rc = c * B + h * HALF
-                    nc.tensor.matmul_mx(
-                        out=acc[:],
-                        lhsT=cg[:, lc : lc + P].bitcast(E5X4),
-                        lhsT_scale=sg[:, lc : lc + P],
-                        rhs=cb[:, rc : rc + HALF].bitcast(E4X4),
-                        rhs_scale=sb[:, rc : rc + HALF],
-                        start=(c == 0),
-                        stop=(c == 1),
-                    )
-                nc.vector.scalar_tensor_tensor(
-                    out=o[:, h * HALF : (h + 1) * HALF],
-                    in0=e_sb[t][:, h * HALF : (h + 1) * HALF],
-                    scalar=0.01,
-                    in1=acc[:],
-                    op0=ALU.max,
-                    op1=ALU.mult,
+            acc = psum_a.tile([P, HALF], F32, name="acc")
+            for c in range(2):
+                lc = ((t % 2) * 2 + c) * P
+                rc = c * B + h * HALF
+                nc.tensor.matmul_mx(
+                    out=acc[:],
+                    lhsT=cg[:, lc : lc + P].bitcast(E5X4),
+                    lhsT_scale=sg[:, lc : lc + P],
+                    rhs=cb[:, rc : rc + HALF].bitcast(E4X4),
+                    rhs_scale=sb[:, rc : rc + HALF],
+                    start=(c == 0),
+                    stop=(c == 1),
                 )
-            nc.sync.dma_start(out=o_v[:, t * B : (t + 1) * B], in_=o[:])
+            acc_ps[(t, h)] = acc
 
-        def masks_first(gr):
-            if gr in MG:
-                clamp_t(gr)
-            else:
-                masks_s(2 * gr)
-                masks_s(2 * gr + 1)
+        def damp(t, h):
+            if h == 0:
+                o_sb[t] = opool.tile([P, B], F32, name="o")
+            nc.vector.scalar_tensor_tensor(
+                out=o_sb[t][:, h * HALF : (h + 1) * HALF],
+                in0=e_sb[t][:, h * HALF : (h + 1) * HALF],
+                scalar=0.01,
+                in1=acc_ps[(t, h)][:],
+                op0=ALU.max,
+                op1=ALU.mult,
+            )
 
-        masks_first(0)
-        bun_prep()
-        g_prep(0)
-        g_prep(1)
-        if 0 in MG:
-            masks_back(0)
-        for gr in range(NG):
-            nxt = gr + 1
-            if nxt < NG:
-                masks_first(nxt)
-                g_prep(2 * nxt)
-                g_prep(2 * nxt + 1)
-            mm_final(GT * gr)
-            mm_final(GT * gr + 1)
-            if nxt < NG and nxt in MG:
-                masks_back(nxt)
-            mm_final(GT * gr + 2)
-            mm_final(GT * gr + 3)
+        def store(t):
+            nc.scalar.dma_start(out=o_v[:, t * B : (t + 1) * B], in_=o_sb[t][:])
+
+        def store_half(t, h):
+            nc.scalar.dma_start(
+                out=o_v[:, t * B + h * HALF : t * B + (h + 1) * HALF], in_=o_sb[t][:, h * HALF : (h + 1) * HALF]
+            )
+
+        def turn_p_half(m):
+            if m < 2 * (NG - 1):
+                for bt in range(4 * (m % 2), 4 * (m % 2) + 4):
+                    turn_p(m // 2 + 1, bt)
+
+        def clamp_half(m):
+            if m < 2 * (NG - 1):
+                for bt in range(4 * (m % 2), 4 * (m % 2) + 4):
+                    clamp(m // 2 + 1, bt)
+
+        for bt in range(NBT):
+            turn_p(0, bt, on_vector=(bt % 2 == 1))
+            clamp(0, bt)
+        for bt in range(NBT):
+            turn_bun(bt, on_vector=(bt % 2 == 1))
+            if bt % 4 == 3:
+                turn_back(bt // 4)
+                in_range(bt // 4)
+                quant_bun(bt // 4)
+        turn_g(0)
+        turn_g(1, on_vector=True)
+        quant_g(0)
+        turn_p_half(0)
+        clamp_half(0)
+
+        for n in range(NPAIR):
+            if n + 1 < NPAIR:
+                turn_g(2 * n + 2)
+                turn_g(2 * n + 3)
+                turn_back(2 * n + 2)
+                turn_back(2 * n + 3)
+            turn_p_half(n + 1)
+            for t in (2 * n, 2 * n + 1):
+                for h in range(2):
+                    multiply(t, h)
+            if n > 0:
+                store(2 * n - 2)
+                store(2 * n - 1)
+            if n + 1 < NPAIR:
+                quant_g(n + 1)
+                in_range(2 * n + 2)
+                in_range(2 * n + 3)
+            clamp_half(n + 1)
+            for t in (2 * n, 2 * n + 1):
+                for h in range(2):
+                    damp(t, h)
+        store(T - 2)
+        store(T - 1)

@@ -10,6 +10,7 @@ U8 = mybir.dt.uint8
 E4X4 = mybir.dt.float8_e4m3fn_x4
 E5X4 = mybir.dt.float8_e5m2_x4
 ALU = mybir.AluOpType
+ACT = mybir.ActivationFunctionType
 
 P = 128
 S = 2048
@@ -21,6 +22,7 @@ NBT = B // P
 HALF = 512
 GT = 4
 NG = T // GT
+MG = (2, 3)
 
 FLOPS = 2 * S * B * K
 BYTES = 2 * S * B + 2 * B * K + 2 * S * K + 4 * B + 4 * S * B
@@ -41,17 +43,22 @@ def tile_optblockv2_t_kernel(
         work = ctx.enter_context(tc.tile_pool(name="work", bufs=3))
         mpool = ctx.enter_context(tc.tile_pool(name="mpool", bufs=2))
         epool = ctx.enter_context(tc.tile_pool(name="epool", bufs=8))
-        opool = ctx.enter_context(tc.tile_pool(name="opool", bufs=6))
+        opool = ctx.enter_context(tc.tile_pool(name="opool", bufs=4))
         psum_t = ctx.enter_context(tc.psum_pool(name="psum_t", bufs=4))
         psum_a = ctx.enter_context(tc.psum_pool(name="psum_a", bufs=4))
-        ctx.enter_context(tc.manual_schedule())
 
+        zrow = const.tile([P, 2 * B], BF16, name="zrow")
+        nc.vector.memset(zrow[:], 0.0)
         rows = const.tile([P, P], BF16, name="rows")
         nc.vector.memset(rows[:], 0.0)
-        identb = const.tile([P, P], BF16, name="identb")
-        make_identity(nc, identb[:])
+        ones = const.tile([P, P], BF16, name="ones")
+        nc.vector.memset(ones[:], 1.0)
         ident = const.tile([P, P], F32, name="ident")
         make_identity(nc, ident[:])
+        identb = const.tile([P, P], BF16, name="identb")
+        make_identity(nc, identb[:])
+        nc.sync.dma_start(out=zrow[0:1, 0:B], in_=avail_bundle.rearrange("(o n) -> o n", o=1))
+        nc.sync.dma_start(out=zrow[0:1, B : 2 * B], in_=alloc_bundle.rearrange("(o n) -> o n", o=1))
         nc.sync.dma_start(out=rows[0:NBT, :], in_=avail_bundle.rearrange("(t p) -> t p", p=P))
         nc.sync.dma_start(out=rows[NBT : 2 * NBT, :], in_=alloc_bundle.rearrange("(t p) -> t p", p=P))
 
@@ -75,13 +82,25 @@ def tile_optblockv2_t_kernel(
         for i in range(NBT // 2):
             nc.sync.dma_start(out=bun_sb[i][:], in_=bun_v[:, 2 * i : 2 * i + 2, :])
         load_g(0)
-        for gr in range(1, NG):
-            load_p(2 * gr)
-            load_p(2 * gr + 1)
-            load_g(2 * gr - 1)
-            load_g(2 * gr)
-        load_g(NPAIR - 1)
+        load_g(1)
+        for i in range(2, NPAIR, 2):
+            load_p(i)
+            load_p(i + 1)
+            load_g(i)
+            load_g(i + 1)
 
+        hi = const.tile([P, B], BF16, name="hi")
+        lo = const.tile([P, B], BF16, name="lo")
+        for j in (2, 3, 0, 1):
+            th = psum_a.tile([P, HALF], F32, name="acc")
+            nc.tensor.matmul(th[:], lhsT=ones[:], rhs=zrow[:, j * HALF : (j + 1) * HALF], start=True, stop=True)
+            if j < 2:
+                nc.scalar.activation(out=hi[:, j * HALF : (j + 1) * HALF], in_=th[:], func=ACT.Relu)
+            else:
+                nc.vector.tensor_scalar(
+                    out=lo[:, (j - 2) * HALF : (j - 1) * HALF], in0=th[:],
+                    scalar1=-1.0, scalar2=0.0, op0=ALU.mult, op1=ALU.min,
+                )
         rt = psum_t.tile([P, P], BF16, name="tp")
         nc.tensor.transpose(rt[:], rows[:], identb[:])
         hi_c = const.tile([P, NBT], F32, name="hi_c")
@@ -91,175 +110,145 @@ def tile_optblockv2_t_kernel(
             out=lo_c[:], in0=rt[:, NBT : 2 * NBT], scalar1=-1.0, scalar2=0.0, op0=ALU.mult, op1=ALU.min
         )
 
+        e_sb = {}
+
         def p_tile(t):
             return p_sb[t // 2][:, (t % 2) * B : (t % 2 + 1) * B]
 
-        def copy_out(on_vector, dst, src):
-            if on_vector:
-                nc.vector.tensor_copy(out=dst, in_=src)
-            else:
-                nc.scalar.copy(out=dst, in_=src)
+        def masks_s(i):
+            ab = []
+            for tt in range(2):
+                pt = p_tile(2 * i + tt)
+                a = mpool.tile([P, B], BF16, name="a%d" % tt)
+                b = mpool.tile([P, B], BF16, name="b%d" % tt)
+                nc.vector.tensor_tensor(out=a[:], in0=pt, in1=hi[:], op=ALU.is_le)
+                nc.vector.tensor_tensor(out=b[:], in0=pt, in1=lo[:], op=ALU.is_ge)
+                ab.append((a, b))
+            for tt in range(2):
+                e = epool.tile([P, B], BF16, name="e")
+                nc.vector.tensor_tensor(out=e[:], in0=ab[tt][0][:], in1=ab[tt][1][:], op=ALU.mult)
+                e_sb[2 * i + tt] = e
 
-        pt_sb = {}
-        ct_sb = {}
-        tc_ps = {}
-        e_sb = {}
-        gg_sb = {}
-        cg_sb = {}
-        acc_ps = {}
-        o_sb = {}
+        c_sb = {}
 
-        def turn_p(gr, bt, on_vector=False):
-            if bt == 0:
-                pt_sb[gr] = mpool.tile([P, NBT, GT * P], BF16, name="p_t")
-                ct_sb[gr] = mpool.tile([P, NBT, GT * P], BF16, name="c_t")
-            tp = psum_t.tile([P, GT * P], BF16, name="tp")
-            for st in range(GT):
-                nc.tensor.transpose(
-                    tp[:, st * P : (st + 1) * P], p_tile(GT * gr + st)[:, bt * P : (bt + 1) * P], identb[:]
-                )
-            copy_out(on_vector, pt_sb[gr][:, bt, :], tp[:])
-
-        def clamp(gr, bt):
-            nc.vector.tensor_scalar(
-                out=ct_sb[gr][:, bt, :], in0=pt_sb[gr][:, bt, :],
-                scalar1=lo_c[:, bt : bt + 1], scalar2=hi_c[:, bt : bt + 1], op0=ALU.max, op1=ALU.min,
-            )
-
-        def turn_back(t):
-            c_t = ct_sb[t // GT]
-            st = t % GT
-            tp = psum_t.tile([P, B], BF16, name="tp")
+        def clamp_t(gr):
+            p_t = mpool.tile([P, NBT, GT * P], BF16, name="p_t")
+            c_t = mpool.tile([P, NBT, GT * P], BF16, name="c_t")
             for bt in range(NBT):
-                nc.tensor.transpose(tp[:, bt * P : (bt + 1) * P], c_t[:, bt, st * P : (st + 1) * P], identb[:])
-            tc_ps[t] = tp
+                tp = psum_t.tile([P, GT * P], BF16, name="tp")
+                for st in range(GT):
+                    nc.tensor.transpose(
+                        tp[:, st * P : (st + 1) * P], p_tile(GT * gr + st)[:, bt * P : (bt + 1) * P], identb[:]
+                    )
+                nc.scalar.copy(out=p_t[:, bt, :], in_=tp[:])
+                nc.vector.tensor_scalar(
+                    out=c_t[:, bt, :], in0=p_t[:, bt, :],
+                    scalar1=lo_c[:, bt : bt + 1], scalar2=hi_c[:, bt : bt + 1], op0=ALU.max, op1=ALU.min,
+                )
+            c_sb[gr] = c_t
 
-        def in_range(t):
-            e = epool.tile([P, B], BF16, name="e")
-            nc.vector.tensor_tensor(out=e[:], in0=tc_ps[t][:], in1=p_tile(t), op=ALU.is_equal)
-            e_sb[t] = e
+        def masks_back(gr):
+            c_t = c_sb[gr]
+            for st in range(GT):
+                tp = psum_t.tile([P, B], BF16, name="tp")
+                for bt in range(NBT):
+                    nc.tensor.transpose(tp[:, bt * P : (bt + 1) * P], c_t[:, bt, st * P : (st + 1) * P], identb[:])
+                e = epool.tile([P, B], BF16, name="e")
+                nc.vector.tensor_tensor(out=e[:], in0=tp[:], in1=p_tile(GT * gr + st), op=ALU.is_equal)
+                e_sb[GT * gr + st] = e
 
         gb = res.tile([P, 2 * B * 4], BF16, name="gb", align_bytes=64)
         gbw = gb[:].bitcast(F32).rearrange("p (c b u) -> p c b u", c=2, b=B, u=2)
         cb = res.tile([P, 2 * B], U32, name="cb", align_bytes=64)
         sb = res.tile([P, 2 * B], U8, name="sb", align_bytes=64)
 
-        def turn_words(words):
+        def turn(words):
             xt = psum_t.tile([P, 4 * P], F32, name="tp")
             for j in range(4):
                 nc.tensor.transpose(xt[:, j * P : (j + 1) * P], words[:, j * P : (j + 1) * P], ident[:])
             return xt[:].rearrange("p (c u w) -> p c w u", c=2, u=2, w=P)
 
-        def turn_bun(bt, on_vector):
-            src = turn_words(bun_sb[bt // 2][:, bt % 2, :].bitcast(F32))
-            copy_out(on_vector, gbw[:, :, bt * P : (bt + 1) * P, :], src)
+        def bun_prep():
+            for bt in range(NBT):
+                words = bun_sb[bt // 2][:, bt % 2, :].bitcast(F32)
+                src = turn(words)
+                nc.scalar.copy(out=gbw[:, :, bt * P : (bt + 1) * P, :], in_=src)
+                if bt % 4 == 3:
+                    h = bt // 4
+                    for c in range(2):
+                        col = c * B + h * HALF
+                        nc.vector.quantize_mx(
+                            out=cb[:, col : col + HALF].bitcast(E4X4),
+                            scales=sb[:, col : col + HALF],
+                            in_=gb[:, 4 * col : 4 * (col + HALF)],
+                        )
 
-        def quant_bun(h):
-            for c in range(2):
-                col = c * B + h * HALF
-                nc.vector.quantize_mx(
-                    out=cb[:, col : col + HALF].bitcast(E4X4),
-                    scales=sb[:, col : col + HALF],
-                    in_=gb[:, 4 * col : 4 * (col + HALF)],
+        cg_sb = {}
+
+        def g_prep(i):
+            gg = work.tile([P, 2 * K], BF16, name="gg", align_bytes=64)
+            ggw = gg[:].bitcast(F32)
+            gw = g_sb[i][:].bitcast(F32)
+            for tt in range(2):
+                src = turn(gw[:, tt * HALF : (tt + 1) * HALF])
+                nc.scalar.copy(
+                    out=ggw[:, tt * HALF : (tt + 1) * HALF].rearrange("p (c w u) -> p c w u", c=2, w=P, u=2),
+                    in_=src,
                 )
-
-        def turn_g(t, on_vector=False):
-            i = t // 2
-            tt = t % 2
-            if tt == 0:
-                gg_sb[i] = work.tile([P, 2 * K], BF16, name="gg", align_bytes=64)
-            src = turn_words(g_sb[i][:].bitcast(F32)[:, tt * HALF : (tt + 1) * HALF])
-            dst = gg_sb[i][:].bitcast(F32)[:, tt * HALF : (tt + 1) * HALF]
-            copy_out(on_vector, dst.rearrange("p (c w u) -> p c w u", c=2, w=P, u=2), src)
-
-        def quant_g(i):
             cg = work.tile([P, HALF], U32, name="cg", align_bytes=64)
             sg = work.tile([P, HALF], U8, name="sg", align_bytes=64)
-            nc.vector.quantize_mx(out=cg[:].bitcast(E5X4), scales=sg[:], in_=gg_sb[i][:])
+            nc.vector.quantize_mx(out=cg[:].bitcast(E5X4), scales=sg[:], in_=gg[:])
             cg_sb[i] = (cg, sg)
 
-        def multiply(t, h):
+        def mm_final(t):
             cg, sg = cg_sb[t // 2]
-            acc = psum_a.tile([P, HALF], F32, name="acc")
-            for c in range(2):
-                lc = ((t % 2) * 2 + c) * P
-                rc = c * B + h * HALF
-                nc.tensor.matmul_mx(
-                    out=acc[:],
-                    lhsT=cg[:, lc : lc + P].bitcast(E5X4),
-                    lhsT_scale=sg[:, lc : lc + P],
-                    rhs=cb[:, rc : rc + HALF].bitcast(E4X4),
-                    rhs_scale=sb[:, rc : rc + HALF],
-                    start=(c == 0),
-                    stop=(c == 1),
+            o = opool.tile([P, B], F32, name="o")
+            for h in range(2):
+                acc = psum_a.tile([P, HALF], F32, name="acc")
+                for c in range(2):
+                    lc = ((t % 2) * 2 + c) * P
+                    rc = c * B + h * HALF
+                    nc.tensor.matmul_mx(
+                        out=acc[:],
+                        lhsT=cg[:, lc : lc + P].bitcast(E5X4),
+                        lhsT_scale=sg[:, lc : lc + P],
+                        rhs=cb[:, rc : rc + HALF].bitcast(E4X4),
+                        rhs_scale=sb[:, rc : rc + HALF],
+                        start=(c == 0),
+                        stop=(c == 1),
+                    )
+                nc.vector.scalar_tensor_tensor(
+                    out=o[:, h * HALF : (h + 1) * HALF],
+                    in0=e_sb[t][:, h * HALF : (h + 1) * HALF],
+                    scalar=0.01,
+                    in1=acc[:],
+                    op0=ALU.max,
+                    op1=ALU.mult,
                 )
-            acc_ps[(t, h)] = acc
+            nc.sync.dma_start(out=o_v[:, t * B : (t + 1) * B], in_=o[:])
 
-        def damp(t, h):
-            if h == 0:
-                o_sb[t] = opool.tile([P, B], F32, name="o")
-            nc.vector.scalar_tensor_tensor(
-                out=o_sb[t][:, h * HALF : (h + 1) * HALF],
-                in0=e_sb[t][:, h * HALF : (h + 1) * HALF],
-                scalar=0.01,
-                in1=acc_ps[(t, h)][:],
-                op0=ALU.max,
-                op1=ALU.mult,
-            )
+        def masks_first(gr):
+            if gr in MG:
+                clamp_t(gr)
+            else:
+                masks_s(2 * gr)
+                masks_s(2 * gr + 1)
 
-        def store(t):
-            nc.scalar.dma_start(out=o_v[:, t * B : (t + 1) * B], in_=o_sb[t][:])
-
-        def store_half(t, h):
-            nc.scalar.dma_start(
-                out=o_v[:, t * B + h * HALF : t * B + (h + 1) * HALF], in_=o_sb[t][:, h * HALF : (h + 1) * HALF]
-            )
-
-        def turn_p_half(m):
-            if m < 2 * (NG - 1):
-                for bt in range(4 * (m % 2), 4 * (m % 2) + 4):
-                    turn_p(m // 2 + 1, bt)
-
-        def clamp_half(m):
-            if m < 2 * (NG - 1):
-                for bt in range(4 * (m % 2), 4 * (m % 2) + 4):
-                    clamp(m // 2 + 1, bt)
-
-        for bt in range(NBT):
-            turn_p(0, bt, on_vector=(bt % 2 == 1))
-            clamp(0, bt)
-        for bt in range(NBT):
-            turn_bun(bt, on_vector=(bt % 2 == 1))
-            if bt % 4 == 3:
-                turn_back(bt // 4)
-                in_range(bt // 4)
-                quant_bun(bt // 4)
-        turn_g(0)
-        turn_g(1, on_vector=True)
-        quant_g(0)
-        turn_p_half(0)
-        clamp_half(0)
-
-        for n in range(NPAIR):
-            if n + 1 < NPAIR:
-                turn_g(2 * n + 2)
-                turn_g(2 * n + 3)
-                turn_back(2 * n + 2)
-                turn_back(2 * n + 3)
-            turn_p_half(n + 1)
-            for t in (2 * n, 2 * n + 1):
-                for h in range(2):
-                    multiply(t, h)
-            if n > 0:
-                store(2 * n - 2)
-                store(2 * n - 1)
-            if n + 1 < NPAIR:
-                quant_g(n + 1)
-                in_range(2 * n + 2)
-                in_range(2 * n + 3)
-            clamp_half(n + 1)
-            for t in (2 * n, 2 * n + 1):
-                for h in range(2):
-                    damp(t, h)
-        store(T - 2)
-        store(T - 1)
+        masks_first(0)
+        bun_prep()
+        g_prep(0)
+        g_prep(1)
+        if 0 in MG:
+            masks_back(0)
+        for gr in range(NG):
+            nxt = gr + 1
+            if nxt < NG:
+                masks_first(nxt)
+                g_prep(2 * nxt)
+                g_prep(2 * nxt + 1)
+            mm_final(GT * gr)
+            mm_final(GT * gr + 1)
+            if nxt < NG and nxt in MG:
+                masks_back(nxt)
+            mm_final(GT * gr + 2)
+            mm_final(GT * gr + 3)

@@ -134,17 +134,21 @@ def tile_optblockv2_t_kernel(
         def clamp_t(gr):
             p_t = mpool.tile([P, NBT, GT * P], BF16, name="p_t")
             c_t = mpool.tile([P, NBT, GT * P], BF16, name="c_t")
-            for bt in range(NBT):
-                tp = psum_t.tile([P, GT * P], BF16, name="tp")
-                for st in range(GT):
-                    nc.tensor.transpose(
-                        tp[:, st * P : (st + 1) * P], p_tile(GT * gr + st)[:, bt * P : (bt + 1) * P], identb[:]
+            for b2 in range(0, NBT, 2):
+                tp = psum_t.tile([P, 2, GT * P], BF16, name="tp")
+                for k in range(2):
+                    for st in range(GT):
+                        nc.tensor.transpose(
+                            tp[:, k, st * P : (st + 1) * P],
+                            p_tile(GT * gr + st)[:, (b2 + k) * P : (b2 + k + 1) * P],
+                            identb[:],
+                        )
+                nc.scalar.copy(out=p_t[:, b2 : b2 + 2, :], in_=tp[:])
+                for bt in (b2, b2 + 1):
+                    nc.vector.tensor_scalar(
+                        out=c_t[:, bt, :], in0=p_t[:, bt, :],
+                        scalar1=lo_c[:, bt : bt + 1], scalar2=hi_c[:, bt : bt + 1], op0=ALU.max, op1=ALU.min,
                     )
-                nc.scalar.copy(out=p_t[:, bt, :], in_=tp[:])
-                nc.vector.tensor_scalar(
-                    out=c_t[:, bt, :], in0=p_t[:, bt, :],
-                    scalar1=lo_c[:, bt : bt + 1], scalar2=hi_c[:, bt : bt + 1], op0=ALU.max, op1=ALU.min,
-                )
             c_sb[gr] = c_t
 
         def masks_back(gr):

@@ -43,6 +43,7 @@ def tile_optblockv2_t_kernel(
         work = ctx.enter_context(tc.tile_pool(name="work", bufs=3))
         mpool = ctx.enter_context(tc.tile_pool(name="mpool", bufs=2))
         epool = ctx.enter_context(tc.tile_pool(name="epool", bufs=8))
+        e2pool = ctx.enter_context(tc.tile_pool(name="e2pool", bufs=4))
         opool = ctx.enter_context(tc.tile_pool(name="opool", bufs=4))
         psum_t = ctx.enter_context(tc.psum_pool(name="psum_t", bufs=4))
         psum_a = ctx.enter_context(tc.psum_pool(name="psum_a", bufs=4))
@@ -110,24 +111,28 @@ def tile_optblockv2_t_kernel(
             out=lo_c[:], in0=rt[:, NBT : 2 * NBT], scalar1=-1.0, scalar2=0.0, op0=ALU.mult, op1=ALU.min
         )
 
+        hi2 = hi[:].rearrange("p (o b) -> p o b", o=1).to_broadcast([P, 2, B])
+        lo2 = lo[:].rearrange("p (o b) -> p o b", o=1).to_broadcast([P, 2, B])
+
         e_sb = {}
 
         def p_tile(t):
             return p_sb[t // 2][:, (t % 2) * B : (t % 2 + 1) * B]
 
-        def masks_s(i):
+        def masks_v(gr):
             ab = []
-            for tt in range(2):
-                pt = p_tile(2 * i + tt)
-                a = mpool.tile([P, B], BF16, name="a%d" % tt)
-                b = mpool.tile([P, B], BF16, name="b%d" % tt)
-                nc.vector.tensor_tensor(out=a[:], in0=pt, in1=hi[:], op=ALU.is_le)
-                nc.vector.tensor_tensor(out=b[:], in0=pt, in1=lo[:], op=ALU.is_ge)
-                ab.append((a, b))
-            for tt in range(2):
-                e = epool.tile([P, B], BF16, name="e")
-                nc.vector.tensor_tensor(out=e[:], in0=ab[tt][0][:], in1=ab[tt][1][:], op=ALU.mult)
-                e_sb[2 * i + tt] = e
+            for i in (2 * gr, 2 * gr + 1):
+                pt = p_sb[i][:].rearrange("p (t b) -> p t b", t=2)
+                a = mpool.tile([P, 2, B], BF16, name="a")
+                b = mpool.tile([P, 2, B], BF16, name="b")
+                nc.vector.tensor_tensor(out=a[:], in0=pt, in1=hi2, op=ALU.is_le)
+                nc.vector.tensor_tensor(out=b[:], in0=pt, in1=lo2, op=ALU.is_ge)
+                ab.append((i, a, b))
+            for i, a, b in ab:
+                e = e2pool.tile([P, 2, B], BF16, name="e2")
+                nc.vector.tensor_tensor(out=e[:], in0=a[:], in1=b[:], op=ALU.mult)
+                for tt in range(2):
+                    e_sb[2 * i + tt] = e[:, tt, :]
 
         c_sb = {}
 
@@ -159,7 +164,7 @@ def tile_optblockv2_t_kernel(
                     nc.tensor.transpose(tp[:, bt * P : (bt + 1) * P], c_t[:, bt, st * P : (st + 1) * P], identb[:])
                 e = epool.tile([P, B], BF16, name="e")
                 nc.vector.tensor_tensor(out=e[:], in0=tp[:], in1=p_tile(GT * gr + st), op=ALU.is_equal)
-                e_sb[GT * gr + st] = e
+                e_sb[GT * gr + st] = e[:]
 
         gb = res.tile([P, 2 * B * 4], BF16, name="gb", align_bytes=64)
         gbw = gb[:].bitcast(F32).rearrange("p (c b u) -> p c b u", c=2, b=B, u=2)
@@ -235,8 +240,7 @@ def tile_optblockv2_t_kernel(
             if gr in MG:
                 clamp_t(gr)
             else:
-                masks_s(2 * gr)
-                masks_s(2 * gr + 1)
+                masks_v(gr)
 
         masks_first(0)
         bun_prep()

from contextlib import ExitStack

import concourse.mybir as mybir
from concourse.masks import make_identity

F32 = mybir.dt.float32
BF16 = mybir.dt.bfloat16
U32 = mybir.dt.uint32
U8 = mybir.dt.uint8
E4X4 = mybir.dt.float8_e4m3fn_x4
E5X4 = mybir.dt.float8_e5m2_x4
ALU = mybir.AluOpType
ACT = mybir.ActivationFunctionType

P = 128
S = 2048
B = 1024
K = 1024
T = S // P
NPAIR = T // 2
NBT = B // P
HALF = 512
GT = 4
NG = T // GT
MG = (2, 3)

FLOPS = 2 * S * B * K
BYTES = 2 * S * B + 2 * B * K + 2 * S * K + 4 * B + 4 * S * B


def tile_optblockv2_t_kernel(
    tc, proba, cur_inven, bun_sc, avail_bundle, alloc_bundle, grad_out, out
):
    nc = tc.nc
    g_v = grad_out.rearrange("o (p x) -> (o p) x", p=P)
    p_v = proba.rearrange("(p x) -> p x", p=P)
    o_v = out.rearrange("(p x) -> p x", p=P)
    bun_v = bun_sc.rearrange("(t p) k -> p t k", p=P)

    with ExitStack() as ctx:
        const = ctx.enter_context(tc.tile_pool(name="const", bufs=1))
        res = ctx.enter_context(tc.tile_pool(name="res", bufs=1))
        work = ctx.enter_context(tc.tile_pool(name="work", bufs=3))
        mpool = ctx.enter_context(tc.tile_pool(name="mpool", bufs=2))
        epool = ctx.enter_context(tc.tile_pool(name="epool", bufs=8))
        e2pool = ctx.enter_context(tc.tile_pool(name="e2pool", bufs=4))
        opool = ctx.enter_context(tc.tile_pool(name="opool", bufs=4))
        psum_t = ctx.enter_context(tc.psum_pool(name="psum_t", bufs=4))
        psum_a = ctx.enter_context(tc.psum_pool(name="psum_a", bufs=4))

        zrow = const.tile([P, 2 * B], BF16, name="zrow")
        nc.vector.memset(zrow[:], 0.0)
        rows = const.tile([P, P], BF16, name="rows")
        nc.vector.memset(rows[:], 0.0)
        ones = const.tile([P, P], BF16, name="ones")
        nc.vector.memset(ones[:], 1.0)
        ident = const.tile([P, P], F32, name="ident")
        make_identity(nc, ident[:])
        identb = const.tile([P, P], BF16, name="identb")
        make_identity(nc, identb[:])
        nc.sync.dma_start(out=zrow[0:1, 0:B], in_=avail_bundle.rearrange("(o n) -> o n", o=1))
        nc.sync.dma_start(out=zrow[0:1, B : 2 * B], in_=alloc_bundle.rearrange("(o n) -> o n", o=1))
        nc.sync.dma_start(out=rows[0:NBT, :], in_=avail_bundle.rearrange("(t p) -> t p", p=P))
        nc.sync.dma_start(out=rows[NBT : 2 * NBT, :], in_=alloc_bundle.rearrange("(t p) -> t p", p=P))

        p_sb = []
        g_sb = []
        bun_sb = []
        for i in range(NPAIR):
            p_sb.append(res.tile([P, 2 * B], BF16, name="p%d" % i))
            g_sb.append(res.tile([P, 2 * K], BF16, name="g%d" % i))
        for i in range(NBT // 2):
            bun_sb.append(res.tile([P, 2, K], BF16, name="bun%d" % i))

        def load_p(i):
            nc.sync.dma_start(out=p_sb[i][:], in_=p_v[:, 2 * B * i : 2 * B * (i + 1)])

        def load_g(i):
            nc.sync.dma_start(out=g_sb[i][:], in_=g_v[:, 2 * K * i : 2 * K * (i + 1)])

        load_p(0)
        load_p(1)
        for i in range(NBT // 2):
            nc.sync.dma_start(out=bun_sb[i][:], in_=bun_v[:, 2 * i : 2 * i + 2, :])
        load_g(0)
        load_g(1)
        for i in range(2, NPAIR, 2):
            load_p(i)
            load_p(i + 1)
            load_g(i)
            load_g(i + 1)

        hi = const.tile([P, B], BF16, name="hi")
        lo = const.tile([P, B], BF16, name="lo")
        for j in (2, 3, 0, 1):
            th = psum_a.tile([P, HALF], F32, name="acc")
            nc.tensor.matmul(th[:], lhsT=ones[:], rhs=zrow[:, j * HALF : (j + 1) * HALF], start=True, stop=True)
            if j < 2:
                nc.scalar.activation(out=hi[:, j * HALF : (j + 1) * HALF], in_=th[:], func=ACT.Relu)
            else:
                nc.vector.tensor_scalar(
                    out=lo[:, (j - 2) * HALF : (j - 1) * HALF], in0=th[:],
                    scalar1=-1.0, scalar2=0.0, op0=ALU.mult, op1=ALU.min,
                )
        rt = psum_t.tile([P, P], BF16, name="tp")
        nc.tensor.transpose(rt[:], rows[:], identb[:])
        hi_c = const.tile([P, NBT], F32, name="hi_c")
        lo_c = const.tile([P, NBT], F32, name="lo_c")
        nc.vector.tensor_scalar_max(out=hi_c[:], in0=rt[:, 0:NBT], scalar1=0.0)
        nc.vector.tensor_scalar(
            out=lo_c[:], in0=rt[:, NBT : 2 * NBT], scalar1=-1.0, scalar2=0.0, op0=ALU.mult, op1=ALU.min
        )

        hi2 = hi[:].rearrange("p (o b) -> p o b", o=1).to_broadcast([P, 2, B])
        lo2 = lo[:].rearrange("p (o b) -> p o b", o=1).to_broadcast([P, 2, B])

        e_sb = {}

        def p_tile(t):
            return p_sb[t // 2][:, (t % 2) * B : (t % 2 + 1) * B]

        def masks_v(gr):
            ab = []
            for i in (2 * gr, 2 * gr + 1):
                pt = p_sb[i][:].rearrange("p (t b) -> p t b", t=2)
                a = mpool.tile([P, 2, B], BF16, name="a")
                b = mpool.tile([P, 2, B], BF16, name="b")
                nc.vector.tensor_tensor(out=a[:], in0=pt, in1=hi2, op=ALU.is_le)
                nc.vector.tensor_tensor(out=b[:], in0=pt, in1=lo2, op=ALU.is_ge)
                ab.append((i, a, b))
            for i, a, b in ab:
                e = e2pool.tile([P, 2, B], BF16, name="e2")
                nc.vector.tensor_tensor(out=e[:], in0=a[:], in1=b[:], op=ALU.mult)
                for tt in range(2):
                    e_sb[2 * i + tt] = e[:, tt, :]

        c_sb = {}

        def clamp_t(gr):
            p_t = mpool.tile([P, NBT, GT * P], BF16, name="p_t")
            c_t = mpool.tile([P, NBT, GT * P], BF16, name="c_t")
            for b2 in range(0, NBT, 2):
                tp = psum_t.tile([P, 2, GT * P], BF16, name="tp")
                for k in range(2):
                    for st in range(GT):
                        nc.tensor.transpose(
                            tp[:, k, st * P : (st + 1) * P],
                            p_tile(GT * gr + st)[:, (b2 + k) * P : (b2 + k + 1) * P],
                            identb[:],
                        )
                nc.scalar.copy(out=p_t[:, b2 : b2 + 2, :], in_=tp[:])
                for bt in (b2, b2 + 1):
                    nc.vector.tensor_scalar(
                        out=c_t[:, bt, :], in0=p_t[:, bt, :],
                        scalar1=lo_c[:, bt : bt + 1], scalar2=hi_c[:, bt : bt + 1], op0=ALU.max, op1=ALU.min,
                    )
            c_sb[gr] = c_t

        def masks_back(gr):
            c_t = c_sb[gr]
            for st in range(GT):
                tp = psum_t.tile([P, B], BF16, name="tp")
                for bt in range(NBT):
                    nc.tensor.transpose(tp[:, bt * P : (bt + 1) * P], c_t[:, bt, st * P : (st + 1) * P], identb[:])
                e = epool.tile([P, B], BF16, name="e")
                nc.vector.tensor_tensor(out=e[:], in0=tp[:], in1=p_tile(GT * gr + st), op=ALU.is_equal)
                e_sb[GT * gr + st] = e[:]

        gb = res.tile([P, 2 * B * 4], BF16, name="gb", align_bytes=64)
        gbw = gb[:].bitcast(F32).rearrange("p (c b u) -> p c b u", c=2, b=B, u=2)
        cb = res.tile([P, 2 * B], U32, name="cb", align_bytes=64)
        sb = res.tile([P, 2 * B], U8, name="sb", align_bytes=64)

        def turn(words):
            xt = psum_t.tile([P, 4 * P], F32, name="tp")
            for j in range(4):
                nc.tensor.transpose(xt[:, j * P : (j + 1) * P], words[:, j * P : (j + 1) * P], ident[:])
            return xt[:].rearrange("p (c u w) -> p c w u", c=2, u=2, w=P)

        def bun_prep():
            for bt in range(NBT):
                words = bun_sb[bt // 2][:, bt % 2, :].bitcast(F32)
                src = turn(words)
                nc.scalar.copy(out=gbw[:, :, bt * P : (bt + 1) * P, :], in_=src)
                if bt % 4 == 3:
                    h = bt // 4
                    for c in range(2):
                        col = c * B + h * HALF
                        nc.vector.quantize_mx(
                            out=cb[:, col : col + HALF].bitcast(E4X4),
                            scales=sb[:, col : col + HALF],
                            in_=gb[:, 4 * col : 4 * (col + HALF)],
                        )

        cg_sb = {}

        def g_prep(i):
            gg = work.tile([P, 2 * K], BF16, name="gg", align_bytes=64)
            ggw = gg[:].bitcast(F32)
            gw = g_sb[i][:].bitcast(F32)
            for tt in range(2):
                src = turn(gw[:, tt * HALF : (tt + 1) * HALF])
                nc.scalar.copy(
                    out=ggw[:, tt * HALF : (tt + 1) * HALF].rearrange("p (c w u) -> p c w u", c=2, w=P, u=2),
                    in_=src,
                )
            cg = work.tile([P, HALF], U32, name="cg", align_bytes=64)
            sg = work.tile([P, HALF], U8, name="sg", align_bytes=64)
            nc.vector.quantize_mx(out=cg[:].bitcast(E5X4), scales=sg[:], in_=gg[:])
            cg_sb[i] = (cg, sg)

        def mm_final(t):
            cg, sg = cg_sb[t // 2]
            o = opool.tile([P, B], F32, name="o")
            for h in range(2):
                acc = psum_a.tile([P, HALF], F32, name="acc")
                for c in range(2):
                    lc = ((t % 2) * 2 + c) * P
                    rc = c * B + h * HALF
                    nc.tensor.matmul_mx(
                        out=acc[:],
                        lhsT=cg[:, lc : lc + P].bitcast(E5X4),
                        lhsT_scale=sg[:, lc : lc + P],
                        rhs=cb[:, rc : rc + HALF].bitcast(E4X4),
                        rhs_scale=sb[:, rc : rc + HALF],
                        start=(c == 0),
                        stop=(c == 1),
                    )
                nc.vector.scalar_tensor_tensor(
                    out=o[:, h * HALF : (h + 1) * HALF],
                    in0=e_sb[t][:, h * HALF : (h + 1) * HALF],
                    scalar=0.01,
                    in1=acc[:],
                    op0=ALU.max,
                    op1=ALU.mult,
                )
            nc.sync.dma_start(out=o_v[:, t * B : (t + 1) * B], in_=o[:])

        def masks_first(gr):
            if gr in MG:
                clamp_t(gr)
            else:
                masks_v(gr)

        masks_first(0)
        bun_prep()
        g_prep(0)
        g_prep(1)
        if 0 in MG:
            masks_back(0)
        for gr in range(NG):
            nxt = gr + 1
            if nxt < NG:
                masks_first(nxt)
                g_prep(2 * nxt)
                g_prep(2 * nxt + 1)
            mm_final(GT * gr)
            mm_final(GT * gr + 1)
            if nxt < NG and nxt in MG:
                masks_back(nxt)
            mm_final(GT * gr + 2)
            mm_final(GT * gr + 3)
